import numpy as np
import ml_dtypes


def mxq(x, axis, fmt="e4m3"):
    dtype, down = {"e4m3": (ml_dtypes.float8_e4m3fn, 7), "e5m2": (ml_dtypes.float8_e5m2, 14)}[fmt]
    v = np.moveaxis(np.asarray(x, np.float32).astype(ml_dtypes.bfloat16).astype(np.float64), axis, -1)
    blocks = v.reshape(v.shape[:-1] + (-1, 32))
    amax = np.abs(blocks).max(-1, keepdims=True)
    byte = np.maximum(np.where(amax > 0, np.frexp(amax)[1] - 1 + 127, 0) - down, 1)
    scale = np.exp2(byte - 127.0)
    codes = (blocks / scale).astype(np.float32).astype(dtype).astype(np.float64)
    return np.moveaxis((codes * scale).reshape(v.shape), -1, axis)


WIDE = False


def mx_kscale(k):
    if not WIDE:
        return np.ones(k)
    levels = np.array([18, -18])
    if k % 512:
        return np.exp2(np.random.permutation(np.resize(levels, k // 32))).repeat(32)
    a = np.empty((k // 512, 16))
    for p in range(k // 512):
        a[p, :8] = np.random.permutation(np.resize(levels, 8))
        for g in range(8):
            far = levels[np.abs(levels - a[p, g]) >= 10]
            a[p, g + 8] = far[np.random.randint(len(far))]
    return np.exp2(a.ravel()).repeat(32)


BF16 = ml_dtypes.bfloat16


def bf(x):
    return np.asarray(x, np.float32).astype(BF16)


def f64(x):
    return np.asarray(x).astype(np.float64)


B, I, H = 512, 1024, 1024
CLOCKS = (0.5, 0.8, 0.95, 0.999)
TWO_PI = 2.0 * np.pi


def sigmoid(v):
    return 1.0 / (1.0 + np.exp(-v))


def setup_inputs():
    s = mx_kscale(B)[:, None]
    u = mx_kscale(H)
    x0 = bf(np.random.standard_normal((B, I)))
    h_state = bf(np.random.standard_normal((B, H)))
    local_angle = bf(np.random.uniform(0.0, TWO_PI, (B, H)))
    persistence = bf(np.repeat(np.asarray(CLOCKS), H // len(CLOCKS)))
    w0 = bf(np.random.standard_normal((I, 3 * H)) * 0.7 / np.sqrt(I))
    weight_hh = bf(np.random.standard_normal((H, 3 * H)) * 0.7 / np.sqrt(H))
    bias = bf(np.random.standard_normal(3 * H) * 0.3)
    gates = f64(x0) @ f64(w0) + f64(h_state) @ f64(weight_hh) + f64(bias)
    g0 = bf(4.0 * np.random.standard_normal((B, H)) * np.exp2(np.random.randint(-6, 1, (B, 1))) / s * u)
    g1 = bf(np.random.standard_normal((B, H)) * np.exp2(np.random.randint(-6, 1, (B, 1))) / s * u)
    return {
        "x": bf(f64(x0) * s),
        "h_state": h_state,
        "local_angle": local_angle,
        "persistence": persistence,
        "weight_ih": bf(f64(w0) / np.tile(u, 3)),
        "weight_hh": weight_hh,
        "bias": bias,
        "gates": np.asarray(gates, np.float32),
        "grad_0": g0,
        "grad_1": g1,
    }


def reference(x, h_state, local_angle, persistence, weight_ih, weight_hh, bias, gates, grad_0, grad_1):
    h = f64(h_state)
    g0 = f64(grad_0)
    g1 = f64(grad_1)
    r_gate, z_gate, n_gate = np.split(f64(gates), 3, axis=-1)
    r = sigmoid(r_gate)
    z = sigmoid(z_gate)
    n = np.tanh(r * n_gate)
    da = g0 * z * (1.0 - n * n)
    dr = da * n_gate * r * (1.0 - r)
    dz = (g0 * (n - h) + TWO_PI * g1) * z * (1.0 - z)
    dn = da * r
    dg = np.concatenate([dr, dz, dn], axis=1)
    dx = mxq(dg, 1, "e5m2") @ mxq(f64(weight_ih), 1, "e4m3").T
    dw = mxq(f64(x), 0, "e4m3").T @ mxq(dg, 0, "e5m2")
    return dx, dw

from contextlib import ExitStack

import concourse.mybir as mybir
from concourse.masks import make_identity

B, I, H = 512, 1024, 1024
FLOPS = 2 * 2 * B * I * 3 * H
BYTES = 4 * B * H * 2 + I * 3 * H * 2 + B * 3 * H * 4 + B * I * 4 + I * 3 * H * 4

F32 = mybir.dt.float32
BF16 = mybir.dt.bfloat16
U32 = mybir.dt.uint32
U8 = mybir.dt.uint8
E4M3 = mybir.dt.float8_e4m3fn_x4
E5M2 = mybir.dt.float8_e5m2_x4
ALU = mybir.AluOpType
ACT = mybir.ActivationFunctionType

P = 128
TWO_PI = 6.283185307179586
HALF = 512
R, Z, N = 0, 1, 2


def tile_yarnixcellv4_pa_v_kernel(
    tc, x, h_state, local_angle, persistence, weight_ih, weight_hh, bias, gates, grad_0, grad_1, out_0, out_1
):
    nc = tc.nc
    gates_v = gates.rearrange("(p j) c -> p j c", j=4)
    g0_v = grad_0.rearrange("(p j) c -> p j c", j=4)
    g1_v = grad_1.rearrange("(p j) c -> p j c", j=4)
    h_v = h_state.rearrange("(p j) c -> p j c", j=4)
    x_v = x.rearrange("(p j) c -> p j c", j=4)
    w_v = weight_ih.rearrange("(s b p) c -> s p b c", s=2, b=4)
    o0_v = out_0.rearrange("(p j) i -> p j i", j=4)
    o1_v = out_1.rearrange("(m p) c -> p m c", p=P)

    with ExitStack() as ctx:
        gp = ctx.enter_context(tc.tile_pool(name="gp", bufs=2))
        tmp = ctx.enter_context(tc.tile_pool(name="tmp", bufs=1))
        keep = ctx.enter_context(tc.tile_pool(name="keep", bufs=1))
        tr = ctx.enter_context(tc.psum_pool(name="tr", bufs=2))
        mm = ctx.enter_context(tc.psum_pool(name="mm", bufs=2))
        op = ctx.enter_context(tc.psum_pool(name="op", bufs=4))
        ctx.enter_context(tc.manual_schedule())

        ident_f = keep.tile([P, P], F32, name="ident_f")
        make_identity(nc, ident_f[:])
        ident_b = keep.tile([P, P], BF16, name="ident_b")
        make_identity(nc, ident_b[:])

        state = {}

        def jsl(jp):
            return slice(2 * jp, 2 * jp + 2)

        def alloc_half(h):
            t = {}
            for nm in ("r", "n", "z"):
                t[nm] = gp.tile([P, 4, HALF], F32, name="g_" + nm, tag="g_" + nm, align_bytes=64)
            for nm in ("g0", "h", "g1"):
                t[nm] = gp.tile([P, 4, HALF], BF16, name="i_" + nm, tag="i_" + nm, align_bytes=64)
            t["N"] = tmp.tile([P, 4, HALF], F32, name="t_n", tag="t_n", bufs=2, align_bytes=64)
            state[h] = t

        def load(h, nm, jp):
            t = state[h]
            js = jsl(jp)
            cs = slice(HALF * h, HALF * h + HALF)
            if nm in ("r", "n", "z"):
                c0 = H * {"r": R, "n": N, "z": Z}[nm] + HALF * h
                src = gates_v[:, js, c0 : c0 + HALF]
            else:
                src = {"g0": g0_v, "g1": g1_v, "h": h_v}[nm][:, js, cs]
            nc.sync.dma_start(out=t[nm][:, js, :], in_=src)

        def sig(h, nm, jp):
            v = state[h][nm][:, jsl(jp), :]
            nc.scalar.activation(out=v, in_=v, func=ACT.Sigmoid)

        def stt(out, in0, scalar, in1, op0, op1):
            nc.vector.scalar_tensor_tensor(out=out, in0=in0, scalar=scalar, in1=in1, op0=op0, op1=op1)

        def op_t(h, jp):
            t = state[h]
            v = t["n"][:, jsl(jp), :]
            stt(v, v, -1.0, t["r"][:, jsl(jp), :], ALU.mult, ALU.mult)

        def op_tanh(h, jp):
            t = state[h]
            nc.scalar.activation(out=t["N"][:, jsl(jp), :], in_=t["n"][:, jsl(jp), :], func=ACT.Tanh, scale=-1.0)

        def op_sq(h, jp):
            t = state[h]
            if jp == 0:
                t["N2"] = tmp.tile([P, 4, HALF], F32, name="t_n2", tag="t_n2", align_bytes=64)
            nc.scalar.activation(out=t["N2"][:, jsl(jp), :], in_=t["N"][:, jsl(jp), :], func=ACT.Square)

        def op_a(h, jp):
            t = state[h]
            s = jsl(jp)
            if jp == 0:
                t["A"] = tmp.tile([P, 4, HALF], F32, name="t_a", tag="t_a", align_bytes=64)
            stt(t["A"][:, s, :], t["g0"][:, s, :], -1.0, t["z"][:, s, :], ALU.mult, ALU.mult)

        def op_zz(h, jp):
            v = state[h]["z"][:, jsl(jp), :]
            stt(v, v, 1.0, v, ALU.subtract, ALU.mult)

        def op_da(h, jp):
            t = state[h]
            s = jsl(jp)
            stt(t["A"][:, s, :], t["N2"][:, s, :], 1.0, t["A"][:, s, :], ALU.subtract, ALU.mult)

        def op_q(h, jp):
            t = state[h]
            s = jsl(jp)
            stt(t["n"][:, s, :], t["r"][:, s, :], 1.0, t["n"][:, s, :], ALU.subtract, ALU.mult)

        def op_e(h, jp):
            t = state[h]
            s = jsl(jp)
            nc.vector.tensor_tensor(out=t["N"][:, s, :], in0=t["h"][:, s, :], in1=t["N"][:, s, :], op=ALU.subtract)

        def op_e2(h, jp):
            t = state[h]
            s = jsl(jp)
            nc.vector.tensor_tensor(out=t["N"][:, s, :], in0=t["g0"][:, s, :], in1=t["N"][:, s, :], op=ALU.mult)

        def op_e3(h, jp):
            t = state[h]
            s = jsl(jp)
            stt(t["N"][:, s, :], t["g1"][:, s, :], -TWO_PI, t["N"][:, s, :], ALU.mult, ALU.add)

        def both(f, h):
            f(h, 0)
            f(h, 1)

        dg = {}

        def final(h, g, a, b, s):
            t = state[h]
            if s == 0:
                dg[(h, g)] = gp.tile([P, 4, P, 4], BF16, name="dgi", tag="dgi", bufs=3, align_bytes=64)

            def v(ap):
                return ap[:, :, 256 * s : 256 * s + 256].rearrange("p j (q t) -> p q j t", t=4)

            nc.vector.tensor_tensor(
                out=dg[(h, g)][:, :, 64 * s : 64 * s + 64, :].rearrange("p t q j -> p q j t"),
                in0=v(t[a]), in1=v(t[b]), op=ALU.mult,
            )

        LATE_TAGS = ('g_n', 'g_z', 'ost', 'ost')
        wc, wnat, wg, banks = {}, {}, {}, {}
        for h in range(2):
            for g in range(3):
                wc[(h, g)] = (
                    keep.tile([P, I], U32, name="wc%d%d" % (h, g), align_bytes=64),
                    keep.tile([P, I], U8, name="ws%d%d" % (h, g), align_bytes=64),
                )

        def load_w(g, s):
            t = gp.tile([P, 4, H], BF16, name="wnat", tag="wnat", bufs=3, align_bytes=64)
            nc.sync.dma_start(out=t[:], in_=w_v[s, :, :, H * g : H * g + H])
            wnat[(g, s)] = t

        def w_turn(g, s, h, bk):
            bank = tr.tile([P, 2, 2, P], F32, name="trw", tag="tr")
            for bb in range(2):
                words = wnat[(g, s)][:, 2 * bk + bb, HALF * h : HALF * h + HALF].bitcast(F32)
                for u in range(2):
                    nc.tensor.transpose(bank[:, bb, u, :], words[:, u : 256 : 2], ident_f[:])
            banks[("w", g, s, h, bk)] = bank

        def copy(eng, out, in_):
            if eng is nc.scalar:
                nc.scalar.copy(out=out, in_=in_)
            else:
                nc.vector.tensor_copy(out=out, in_=in_)

        def w_copy(eng, g, s, h, bk):
            if (g, s, h) not in wg:
                wg[(g, s, h)] = gp.tile([P, HALF * 4], BF16, name="wg", tag="wg", bufs=3, align_bytes=64)
            dst = wg[(g, s, h)][:].bitcast(F32).rearrange("p (b r u) -> p b r u", b=4, u=2)
            copy(eng, dst[:, 2 * bk : 2 * bk + 2], banks[("w", g, s, h, bk)][:].rearrange("p b u r -> p b r u"))

        def w_quant(g, s, h):
            codes, scales = wc[(h, g)]
            cs = slice(HALF * s, HALF * s + HALF)
            nc.vector.quantize_mx(out=codes[:, cs].bitcast(E4M3), scales=scales[:, cs], in_=wg[(g, s, h)][:])

        xc = keep.tile([P, I], U32, name="xc", align_bytes=64)
        xs = keep.tile([P, I], U8, name="xs", align_bytes=64)
        xg = {}

        def load_x(s):
            state[("x", s)] = gp.tile([P, 4, HALF], BF16, name="xnat", tag="dgi", bufs=3, align_bytes=64)
            nc.sync.dma_start(out=state[("x", s)][:], in_=x_v[:, :, HALF * s : HALF * s + HALF])

        def x_weave(s):
            xg[s] = gp.tile([P, HALF * 4], BF16, name="xg", tag="dt", align_bytes=64)
            nc.vector.tensor_copy(
                out=xg[s][:].rearrange("p (c i j) -> p c j i", i=4, j=4),
                in_=state[("x", s)][:].rearrange("p j (c i) -> p c j i", i=4),
            )

        def x_quant(s):
            cs = slice(HALF * s, HALF * s + HALF)
            nc.vector.quantize_mx(out=xc[:, cs].bitcast(E4M3), scales=xs[:, cs], in_=xg[s][:])

        tokc, dtc, dt, ost, groups = {}, {}, {}, {}, {}

        def tok_quant(h, g):
            codes = gp.tile([P, HALF], U32, name="tokc", tag="tokc", align_bytes=64)
            scales = gp.tile([P, HALF], U8, name="toks", tag="toks", align_bytes=64)
            nc.vector.quantize_mx(out=codes[:].bitcast(E5M2), scales=scales[:], in_=dg[(h, g)][:].rearrange("p t q j -> p (t q j)"))
            tokc[(h, g)] = (codes, scales)

        def dg_turn(h, g, jp):
            bank = tr.tile([P, 2, 4, P], BF16, name="trd", tag="tr")
            for jj in range(2):
                for t in range(4):
                    nc.tensor.transpose(bank[:, jj, t, :], dg[(h, g)][:, t, :, 2 * jp + jj], ident_b[:])
            banks[("d", h, g, jp)] = bank

        def dg_copy(eng, h, g, jp):
            if (h, g) not in dt:
                dt[(h, g)] = gp.tile([P, 4 * P * 4], BF16, name="dt", tag="dt", align_bytes=64)
            dst = dt[(h, g)][:].rearrange("q (j p t) -> q j p t", j=4, t=4)
            copy(eng, dst[:, 2 * jp : 2 * jp + 2], banks[("d", h, g, jp)][:].rearrange("q j t p -> q j p t"))

        def dg_quant(h, g):
            codes = keep.tile([P, HALF], U32, name="dtc%d%d" % (h, g), align_bytes=64)
            scales = keep.tile([P, HALF], U8, name="dts%d%d" % (h, g), align_bytes=64)
            nc.vector.quantize_mx(out=codes[:].bitcast(E5M2), scales=scales[:], in_=dt[(h, g)][:])
            dtc[(h, g)] = (codes, scales)

        def o1_mm(h, g, m):
            codes, scales = tokc[(h, g)]
            ms = slice(P * m, P * m + P)
            acc = mm.tile([P, HALF], F32, name="acc", tag="acc")
            nc.tensor.matmul_mx(
                out=acc[:], lhsT=xc[:, ms].bitcast(E4M3), lhsT_scale=xs[:, ms],
                rhs=codes[:].bitcast(E5M2), rhs_scale=scales[:], start=True, stop=True,
            )
            banks[("o1", h, g, m)] = acc

        done = {}

        def stage(key, tag):
            if key not in ost:
                if tag == "ost":
                    ost[key] = gp.tile([P, 2, HALF], F32, name="ost", tag="ost", bufs=5, align_bytes=64)[:, :, :]
                else:
                    ost[key] = gp.tile([P, 4, HALF], F32, name="late", tag=tag, align_bytes=64)[:, 0:2, :]
                done[key] = 0
            return ost[key]

        def o1_copy(eng, h, g, m):
            c0 = H * g + HALF * h
            key = (h, g, m // 2)
            tag = "ost"
            if (h, g) == (1, Z):
                tag = LATE_TAGS[m // 2]
            st = stage(key, tag)
            copy(eng, st[:, m % 2, :].rearrange("p (q t) -> p q t", t=4), banks[("o1", h, g, m)][:].rearrange("p (t q) -> p q t", t=4))
            done[key] += 1
            if done[key] == 2:
                m0 = m - m % 2
                nc.sync.dma_start(out=o1_v[:, m0 : m0 + 2, c0 : c0 + HALF], in_=st)

        order = [(0, N), (0, R), (0, Z), (1, N), (1, R), (1, Z)]

        def o0_mm(j, s, ks, start, stop):
            if start:
                late = (j, s) in late_groups and not stop
                groups[(j, s)] = (tr if late else op).tile([P, HALF], F32, name="acc0", tag="tr" if late else "acc0")
            js, cs = slice(P * j, P * j + P), slice(HALF * s, HALF * s + HALF)
            for k in ks:
                codes, scales = dtc[order[k]]
                wcodes, wscales = wc[order[k]]
                nc.tensor.matmul_mx(
                    out=groups[(j, s)][:], lhsT=codes[:, js].bitcast(E5M2), lhsT_scale=scales[:, js],
                    rhs=wcodes[:, cs].bitcast(E4M3), rhs_scale=wscales[:, cs],
                    start=start and k == ks[0], stop=stop and k == ks[-1],
                )

        part = {}
        late_groups = ((2, 0), (2, 1))

        def o0_dump(eng, j, s):
            if "t" not in part:
                part["t"] = gp.tile([P, 4, HALF], F32, name="part", tag="g_r", align_bytes=64)
            part[(j, s)] = part["t"][:, 2 * (j % 2) + s, :]
            copy(eng, part[(j, s)], groups[(j, s)][:])

        def o0_copy(eng, j, s):
            st = stage(("o0", j), "ost")
            if (j, s) in part:
                nc.vector.tensor_tensor(out=st[:, s, :], in0=groups[(j, s)][:], in1=part[(j, s)], op=ALU.add)
            else:
                copy(eng, st[:, s, :], groups[(j, s)][:])
            done[("o0", j)] += 1
            if done[("o0", j)] == 2:
                nc.sync.dma_start(out=o0_v[:, j, :], in_=st.rearrange("p s i -> p (s i)"))

        vq, sq, pq = [], [], []
        seen = set()

        def put(queue, key, needs, fn, *args):
            queue.append((key, needs, fn, args))

        def issue():
            heads = [0, 0, 0]
            moved = True
            while moved:
                moved = False
                for i, queue in enumerate((sq, vq, pq)):
                    if heads[i] < len(queue):
                        key, needs, fn, args = queue[heads[i]]
                        if all(n in seen for n in needs):
                            fn(*args)
                            seen.add(key)
                            heads[i] += 1
                            moved = True
            assert heads == [len(sq), len(vq), len(pq)], [q[k][0] for q, k in zip((sq, vq, pq), heads) if k < len(q)]

        alloc_half(0)
        alloc_half(1)
        for jp in range(2):
            for nm in ("r", "n", "z", "g0"):
                load(0, nm, jp)
        load_x(0)
        load_w(N, 0)
        load_x(1)
        load_w(N, 1)
        load_w(R, 0)
        for nm in ("h", "g1"):
            both(lambda h, jp: load(h, nm, jp), 0)

        def ve(name, f, h, jp, needs=()):
            put(vq, (name, h, jp), needs, f, h, jp)

        def v_t(h, jp): ve("T", op_t, h, jp, [("sr", h, jp)])
        def v_a(h, jp): ve("A", op_a, h, jp, [("sz", h, jp)])
        def v_da(h, jp): ve("DA", op_da, h, jp, [("sq", h, jp)])
        def v_q(h, jp): ve("Q", op_q, h, jp, [("th", h, jp)])
        def v_zz(h, jp): ve("ZZ", op_zz, h, jp)
        def v_e(h, jp): ve("E", op_e, h, jp, [("sq", h, jp)])
        def v_e2(h, jp): ve("E2", op_e2, h, jp)
        def v_e3(h, jp): ve("E3", op_e3, h, jp)

        def v_fin(h, g, s):
            a, b = {N: ("A", "r"), R: ("A", "n"), Z: ("N", "z")}[g]
            put(vq, ("F", h, g, s), (), final, h, g, a, b, s)

        def v_tok(h, g): put(vq, ("tok", h, g), (), tok_quant, h, g)
        def v_dtq(h, g): put(vq, ("dtq", h, g), [("dc", h, g, 0), ("dc", h, g, 1)], dg_quant, h, g)
        def v_wq(g, s, h): put(vq, ("wq", g, s, h), [("wcp", g, s, h, 0), ("wcp", g, s, h, 1)], w_quant, g, s, h)

        def s_r(h, jp): put(sq, ("sr", h, jp), (), sig, h, "r", jp)
        def s_z(h, jp): put(sq, ("sz", h, jp), (), sig, h, "z", jp)
        def s_th(h, jp): put(sq, ("th", h, jp), [("T", h, jp)], op_tanh, h, jp)
        def s_sq(h, jp): put(sq, ("sq", h, jp), (), op_sq, h, jp)

        tr_keys, mm_keys, op_keys = [], [], []
        TRB, MMB = 2, 2

        def q_of(eng):
            return sq if eng is nc.scalar else vq

        def c_w(g, s, h, eng=nc.scalar, after=None):
            for bk in range(2):
                need = [tr_keys[-TRB]] if len(tr_keys) >= TRB else []
                put(pq, ("wt", g, s, h, bk), need, w_turn, g, s, h, bk)
                key = ("wcp", g, s, h, bk)
                put(q_of(eng), key, [("wt", g, s, h, bk)], w_copy, eng, g, s, h, bk)
                tr_keys.append(key)
            if after is not None:
                put(pq, ("lw",) + after, (), load_w, *after)

        def c_d(h, g, engs=(nc.scalar, nc.scalar)):
            for jp in range(2):
                need = [tr_keys[-TRB]] if len(tr_keys) >= TRB else []
                put(pq, ("dtn", h, g, jp), need + [("F", h, g, 1)], dg_turn, h, g, jp)
                key = ("dc", h, g, jp)
                put(q_of(engs[jp]), key, [("dtn", h, g, jp)], dg_copy, engs[jp], h, g, jp)
                tr_keys.append(key)

        def c_o1(h, g, ms, eng=nc.scalar, banks_free=None):
            nb = banks_free or MMB
            for m in ms:
                need = [mm_keys[-nb]] if len(mm_keys) >= nb else []
                put(pq, ("o1m", h, g, m), need + [("tok", h, g), ("xq", 1)], o1_mm, h, g, m)
                e = eng if eng is not None else (nc.scalar, nc.vector)[m % 2]
                key = ("o1c", h, g, m)
                put(q_of(e), key, [("o1m", h, g, m)], o1_copy, e, h, g, m)
                mm_keys.append(key)

        def p_o0(j, s, ks, start, stop):
            need = []
            if start and not stop and (j, s) in late_groups:
                need = [tr_keys[-TRB]]
                tr_keys.append(("o0c", j, s))
            elif start and len(op_keys) >= 4:
                need = [op_keys[-4]]
            for k in ks:
                h, g = order[k]
                need = need + [("dtq", h, g), ("wq", g, s, h)]
            put(pq, ("o0m", j, s, start, stop), need, o0_mm, j, s, list(ks), start, stop)

        def c_dump(j, s, eng=nc.scalar):
            key = ("o0d", j, s)
            put(q_of(eng), key, [("o0m", j, s, True, True)], o0_dump, eng, j, s)
            op_keys.append(key)

        def c_o0(j, s, eng, keym):
            key = ("o0c", j, s)
            put(q_of(eng), key, [("o0m", j, s) + keym], o0_copy, eng, j, s)
            if (j, s) not in late_groups:
                op_keys.append(key)


        def two(f, h):
            f(h, 0)
            f(h, 1)

        def xw(s): put(vq, ("xw", s), (), x_weave, s)
        def xq(s): put(vq, ("xq", s), (), x_quant, s)

        v_t(0, 0); v_a(0, 0); v_q(0, 0); v_t(0, 1); v_da(0, 0); v_a(0, 1)
        xw(0); v_q(0, 1); v_da(0, 1); xw(1); xq(0)
        v_fin(0, N, 0); v_fin(0, N, 1)
        xq(1)
        v_tok(0, N)
        v_fin(0, R, 0); v_fin(0, R, 1)
        v_wq(N, 0, 0)
        v_tok(0, R)
        v_wq(N, 0, 1)
        two(v_zz, 0)
        two(v_e, 0)
        v_wq(N, 1, 0)
        two(v_e2, 0)
        v_wq(N, 1, 1)
        two(v_e3, 0)
        v_wq(R, 0, 0)
        v_dtq(0, N)
        v_fin(0, Z, 0); v_fin(0, Z, 1)
        v_wq(R, 0, 1)
        two(v_t, 1)
        v_tok(0, Z)
        two(v_a, 1)
        v_dtq(0, R)
        two(v_da, 1)
        v_fin(1, N, 0); v_fin(1, N, 1)
        v_tok(1, N)
        two(v_q, 1)
        v_fin(1, R, 0); v_fin(1, R, 1)
        v_wq(R, 1, 0)
        v_tok(1, R)
        v_dtq(0, Z)
        two(v_e, 1)
        v_wq(R, 1, 1)
        v_wq(Z, 0, 0)
        two(v_e2, 1)
        v_wq(Z, 0, 1)
        two(v_zz, 1)
        two(v_e3, 1)
        v_dtq(1, N)
        v_wq(Z, 1, 0)
        v_fin(1, Z, 0)
        v_wq(Z, 1, 1)
        v_fin(1, Z, 1)
        v_dtq(1, R)
        v_tok(1, Z)

        def ld(*nms):
            for nm in nms:
                for jp in range(2):
                    put(pq, ("ld", nm, jp), (), load, 1, nm, jp)

        def lw(g, s): put(pq, ("lw", g, s), (), load_w, g, s)

        s_r(0, 0); s_z(0, 0); s_th(0, 0); s_r(0, 1); s_sq(0, 0); s_z(0, 1); s_th(0, 1); s_sq(0, 1)
        c_w(N, 0, 0); c_w(N, 0, 1); c_w(N, 1, 0); c_w(N, 1, 1); c_w(R, 0, 0); c_w(R, 0, 1)
        ld("r", "n")
        c_o1(0, N, range(4))
        ld("z")
        c_o1(0, N, range(4, 8))
        c_d(0, N)
        ld("g0")
        c_o1(0, R, range(4))
        c_o1(0, R, range(4, 8))
        two(s_r, 1)
        lw(R, 1)
        two(s_z, 1)
        c_d(0, R)
        ld("h", "g1")
        two(s_th, 1)
        lw(Z, 0)
        two(s_sq, 1)
        c_w(R, 1, 0); c_w(R, 1, 1)
        lw(Z, 1)
        c_o1(0, Z, range(8))
        c_d(0, Z)
        c_w(Z, 0, 0); c_w(Z, 0, 1)
        for m in range(8):
            c_o1(1, N, [m])
            if m in (1, 3):
                j = 2 + m // 2
                p_o0(j, 0, [0, 1, 2], True, True)
                c_dump(j, 0)
            if m in (5, 7):
                p_o0(m // 2 - 2, 0, [0, 1, 2], True, False)
        c_d(1, N)
        c_w(Z, 1, 0); c_w(Z, 1, 1)
        c_d(1, R)
        for m in range(4):
            c_o1(1, R, [m])
            if m in (1, 3):
                j = 2 + m // 2
                p_o0(j, 1, [0, 1, 2], True, True)
                c_dump(j, 1)
        for j in (0, 1):
            p_o0(j, 0, [3, 4], False, False)
        c_d(1, Z, (nc.scalar, nc.vector))
        v_dtq(1, Z)
        for m in range(4, 8):
            c_o1(1, R, [m], eng=None)
            if m in (5, 7):
                p_o0(m // 2 - 2, 1, [0, 1, 2, 3, 4], True, False)
        for s in (0, 1):
            p_o0(2, s, [3, 4], True, False)
        c_o1(1, Z, range(4), eng=None)
        for j in (0, 1):
            for s in (0, 1):
                p_o0(j, s, [5], False, True)
                c_o0(j, s, (nc.scalar, nc.vector)[s], (False, True))
        for s in (0, 1):
            p_o0(2, s, [5], False, True)
            c_o0(2, s, nc.vector, (False, True))
        for s in (0, 1):
            p_o0(3, s, [3, 4, 5], True, True)
            c_o0(3, s, nc.vector, (True, True))
        c_o1(1, Z, range(4, 8), eng=nc.scalar)

        issue()
